import numpy as np
import ml_dtypes

BF16 = ml_dtypes.bfloat16


def bf(x):
    return np.asarray(x, np.float32).astype(BF16)


def f32(x):
    return np.asarray(x, np.float32)


def f64(x):
    return np.asarray(x).astype(np.float64)


def striped(idx):
    return np.tile(idx.reshape(-1, 16).T, (8, 1))


D, F, S, T, R, N, P = 512, 512, 2048, 2048, 3, 6144, 1024
CS = 1.0 / np.sqrt(R + 1.0)
CT = 1.0 / (R + 1.0)


def glorot(a, b):
    lim = np.sqrt(6.0 / (a + b))
    return f32(np.random.uniform(-lim, lim, (a, b)))


def setup_inputs():
    return {
        "xs": f32(np.random.standard_normal((D, S))),
        "xt": f32(np.random.standard_normal((D, T))),
        "w1": glorot(D, F),
        "b1": f32(0.1 * np.random.standard_normal((F, 1))),
        "w2": glorot(F, F),
        "offs": striped(np.concatenate([np.random.permutation(S)[:P] for _ in range(N // P)])),
    }


def reference(xs, xt, w1, b1, w2, offs):
    idx = offs[:16].T.reshape(-1)
    ys = f64(w1).T @ f64(xs)
    yt = f64(w1).T @ f64(xt)
    acc = (CT / CS) * yt
    for r in range(R):
        acc = ys[:, idx[r * T:(r + 1) * T]] + acc
    hs = np.maximum(ys + f64(b1), 0.0)
    ht = np.maximum(CS * acc + f64(b1), 0.0)
    return np.concatenate([f64(w2).T @ hs, f64(w2).T @ ht], axis=1)

@@ -1,0 +1,119 @@
+import concourse.mybir as mybir
+
+F32 = mybir.dt.float32
+BF16 = mybir.dt.bfloat16
+U16 = mybir.dt.uint16
+ADD = mybir.AluOpType.add
+RELU = mybir.ActivationFunctionType.Relu
+COPY = mybir.ActivationFunctionType.Copy
+
+P = 128
+FEATURES = 512
+NODES = 2048
+SOURCES = 3
+BLOCKS = FEATURES // P
+CHUNK = 512
+CHUNKS = NODES // CHUNK
+LIST = SOURCES * NODES
+
+FLOPS = 2 * 2 * FEATURES * FEATURES * 2 * NODES
+
+
+def tile_perception_b_kernel(tc, xs, xt, w1, b1, w2, offs, out):
+    nc = tc.nc
+    with (
+        tc.tile_pool(name="held", bufs=1) as held,
+        tc.tile_pool(name="halves", bufs=2 * BLOCKS) as halves,
+        tc.tile_pool(name="sums", bufs=4) as sums,
+        tc.tile_pool(name="results", bufs=4) as results,
+        tc.psum_pool(name="psum", bufs=4) as psum,
+    ):
+        offsets = held.tile([P, LIST // 16], U16, name="offsets")
+        nc.sync.dma_start(offsets[:], offs)
+
+        bias = held.tile([P, BLOCKS, 1], F32, name="bias")
+        with nc.allow_non_contiguous_dma(reason="one bias value to a partition"):
+            nc.scalar.dma_start(bias[:], b1.rearrange("(f p) o -> p f o", p=P))
+
+        def load(view, name):
+            raw = held.tile([P, BLOCKS, CHUNK], F32, name=name)
+            nc.sync.dma_start(raw[:], view)
+            return raw
+
+        xs_view = xs.rearrange("(k p) s -> p k s", p=P)
+        xt_view = xt.rearrange("(k p) t -> p k t", p=P)
+        w1_raw = load(w1.rearrange("(k p) f -> p k f", p=P), "w1_raw")
+        xs_raw = [load(xs_view[:, :, c * CHUNK : (c + 1) * CHUNK], f"xs_raw{c}") for c in range(CHUNKS)]
+        xt_raw = [load(xt_view[:, :, c * CHUNK : (c + 1) * CHUNK], f"xt_raw{c}") for c in range(2)]
+        w2_raw = load(w2.rearrange("(f p) m -> p f m", p=P), "w2_raw")
+        xt_raw += [load(xt_view[:, :, c * CHUNK : (c + 1) * CHUNK], f"xt_raw{c}") for c in range(2, CHUNKS)]
+
+        w1_bf = held.tile([P, BLOCKS, FEATURES], BF16, name="w1_bf")
+        w2_bf = held.tile([P, BLOCKS, FEATURES], BF16, name="w2_bf")
+        xs_bf = [held.tile([P, BLOCKS, CHUNK], BF16, name=f"xs_bf{c}") for c in range(CHUNKS)]
+        xt_bf = [held.tile([P, BLOCKS, CHUNK], BF16, name=f"xt_bf{c}") for c in range(CHUNKS)]
+        hs = [held.tile([P, BLOCKS, CHUNK], BF16, name=f"hs{c}") for c in range(CHUNKS)]
+        ht = [held.tile([P, BLOCKS, CHUNK], BF16, name=f"ht{c}") for c in range(CHUNKS)]
+        ys = [held.tile([P, NODES], F32, name=f"ys{f}") for f in range(BLOCKS)]
+
+        def project(x_bf, f):
+            bank = psum.tile([P, CHUNK], F32, name="projected")
+            for k in range(BLOCKS):
+                nc.tensor.matmul(
+                    bank[:], w1_bf[:, k, f * P : (f + 1) * P], x_bf[:, k, :],
+                    start=(k == 0), stop=(k == BLOCKS - 1),
+                )
+            return bank
+
+        def project_sources(c):
+            nc.vector.tensor_copy(xs_bf[c][:], xs_raw[c][:])
+            for f in range(BLOCKS):
+                bank = project(xs_bf[c], f)
+                ys_chunk = ys[f][:, c * CHUNK : (c + 1) * CHUNK]
+                nc.vector.tensor_copy(ys_chunk, bank[:])
+                nc.scalar.activation(hs[c][:, f, :], ys_chunk, RELU, bias=bias[:, f, :])
+
+        def project_targets(c):
+            nc.scalar.activation(xt_bf[c][:], xt_raw[c][:], COPY)
+            started = []
+            for f in range(BLOCKS):
+                bank = project(xt_bf[c], f)
+                half = halves.tile([P, CHUNK], F32, name="half")
+                nc.scalar.activation(half[:], bank[:], COPY, scale=0.5)
+                started.append(half)
+            return started
+
+        def aggregate(c, started):
+            for f in range(BLOCKS):
+                total = started[f]
+                for r in range(SOURCES):
+                    first = (r * NODES + c * CHUNK) // 16
+                    picked = ys[f][:].indirect(offsets[:, first : first + CHUNK // 16])
+                    longer = sums.tile([P, CHUNK], F32, name="longer")
+                    nc.vector.tensor_tensor(longer[:], picked, total[:], ADD)
+                    total = longer
+                nc.scalar.activation(ht[c][:, f, :], total[:], RELU, bias=bias[:, f, :], scale=0.5)
+
+        def second_layer(h, first_column):
+            for m in range(BLOCKS):
+                bank = psum.tile([P, CHUNK], F32, name="product")
+                for f in range(BLOCKS):
+                    nc.tensor.matmul(
+                        bank[:], w2_bf[:, f, m * P : (m + 1) * P], h[:, f, :],
+                        start=(f == 0), stop=(f == BLOCKS - 1),
+                    )
+                result = results.tile([P, CHUNK], F32, name="result")
+                nc.scalar.activation(result[:], bank[:], COPY)
+                nc.sync.dma_start(out[m * P : (m + 1) * P, first_column : first_column + CHUNK], result[:])
+
+        nc.vector.tensor_copy(w1_bf[:], w1_raw[:])
+        for c in range(CHUNKS):
+            project_sources(c)
+        started = project_targets(0)
+        nc.scalar.activation(w2_bf[:], w2_raw[:], COPY)
+        for c in range(CHUNKS):
+            following = project_targets(c + 1) if c + 1 < CHUNKS else None
+            aggregate(c, started)
+            second_layer(hs[c], c * CHUNK)
+            second_layer(ht[c], NODES + c * CHUNK)
+            started = following

@@ -15,6 +15,9 @@ BLOCKS = FEATURES // P
 CHUNK = 512
 CHUNKS = NODES // CHUNK
 LIST = SOURCES * NODES
+PIECES = 2
+PIECE = CHUNK // PIECES
+EARLY = 2
 
 FLOPS = 2 * 2 * FEATURES * FEATURES * 2 * NODES
 
@@ -23,10 +26,11 @@ def tile_perception_b_kernel(tc, xs, xt, w1, b1, w2, offs, out):
     nc = tc.nc
     with (
         tc.tile_pool(name="held", bufs=1) as held,
-        tc.tile_pool(name="halves", bufs=2 * BLOCKS) as halves,
-        tc.tile_pool(name="sums", bufs=4) as sums,
-        tc.tile_pool(name="results", bufs=4) as results,
-        tc.psum_pool(name="psum", bufs=4) as psum,
+        tc.tile_pool(name="partials", bufs=2 * PIECES) as partials,
+        tc.tile_pool(name="relus", bufs=2) as relus,
+        tc.tile_pool(name="results", bufs=6) as results,
+        tc.psum_pool(name="banks", bufs=4) as banks,
+        tc.psum_pool(name="open_banks", bufs=1) as open_banks,
     ):
         offsets = held.tile([P, LIST // 16], U16, name="offsets")
         nc.sync.dma_start(offsets[:], offs)
@@ -35,29 +39,39 @@ def tile_perception_b_kernel(tc, xs, xt, w1, b1, w2, offs, out):
         with nc.allow_non_contiguous_dma(reason="one bias value to a partition"):
             nc.scalar.dma_start(bias[:], b1.rearrange("(f p) o -> p f o", p=P))
 
-        def load(view, name):
-            raw = held.tile([P, BLOCKS, CHUNK], F32, name=name)
-            nc.sync.dma_start(raw[:], view)
-            return raw
-
-        xs_view = xs.rearrange("(k p) s -> p k s", p=P)
-        xt_view = xt.rearrange("(k p) t -> p k t", p=P)
-        w1_raw = load(w1.rearrange("(k p) f -> p k f", p=P), "w1_raw")
-        xs_raw = [load(xs_view[:, :, c * CHUNK : (c + 1) * CHUNK], f"xs_raw{c}") for c in range(CHUNKS)]
-        xt_raw = [load(xt_view[:, :, c * CHUNK : (c + 1) * CHUNK], f"xt_raw{c}") for c in range(2)]
-        w2_raw = load(w2.rearrange("(f p) m -> p f m", p=P), "w2_raw")
-        xt_raw += [load(xt_view[:, :, c * CHUNK : (c + 1) * CHUNK], f"xt_raw{c}") for c in range(2, CHUNKS)]
+        w1_blocks = w1.rearrange("(k p) f -> p k f", p=P)
+        w2_blocks = w2.rearrange("(f p) m -> p f m", p=P)
+        xs_blocks = xs.rearrange("(k p) s -> p k s", p=P)
+        xt_blocks = xt.rearrange("(k p) t -> p k t", p=P)
+        w1_raw = held.tile([P, BLOCKS, FEATURES], F32, name="w1_raw")
+        w2_raw = held.tile([P, BLOCKS, FEATURES], F32, name="w2_raw")
+        xs_raw = [held.tile([P, BLOCKS, CHUNK], F32, name=f"xs_raw{c}") for c in range(CHUNKS)]
+        xt_raw = [held.tile([P, BLOCKS, CHUNK], F32, name=f"xt_raw{c}") for c in range(CHUNKS)]
+        for k in range(BLOCKS):
+            nc.sync.dma_start(w1_raw[:, k, :], w1_blocks[:, k, :])
+            nc.sync.dma_start(xt_raw[0][:, k, :], xt_blocks[:, k, 0:CHUNK])
+        for c in range(CHUNKS):
+            nc.sync.dma_start(xs_raw[c][:], xs_blocks[:, :, c * CHUNK : (c + 1) * CHUNK])
+        for c in range(1, CHUNKS):
+            nc.sync.dma_start(xt_raw[c][:], xt_blocks[:, :, c * CHUNK : (c + 1) * CHUNK])
+        nc.sync.dma_start(w2_raw[:], w2_blocks)
 
         w1_bf = held.tile([P, BLOCKS, FEATURES], BF16, name="w1_bf")
         w2_bf = held.tile([P, BLOCKS, FEATURES], BF16, name="w2_bf")
         xs_bf = [held.tile([P, BLOCKS, CHUNK], BF16, name=f"xs_bf{c}") for c in range(CHUNKS)]
         xt_bf = [held.tile([P, BLOCKS, CHUNK], BF16, name=f"xt_bf{c}") for c in range(CHUNKS)]
         hs = [held.tile([P, BLOCKS, CHUNK], BF16, name=f"hs{c}") for c in range(CHUNKS)]
-        ht = [held.tile([P, BLOCKS, CHUNK], BF16, name=f"ht{c}") for c in range(CHUNKS)]
         ys = [held.tile([P, NODES], F32, name=f"ys{f}") for f in range(BLOCKS)]
+        totals = [
+            [held.tile([P, CHUNK], F32, name=f"total{c}_{f}") for f in range(BLOCKS)] for c in range(CHUNKS)
+        ]
+
+        def round_by_block(rounded, raw):
+            for k in range(BLOCKS):
+                nc.vector.tensor_copy(rounded[:, k, :], raw[:, k, :])
 
         def project(x_bf, f):
-            bank = psum.tile([P, CHUNK], F32, name="projected")
+            bank = banks.tile([P, CHUNK], F32, name="bank")
             for k in range(BLOCKS):
                 nc.tensor.matmul(
                     bank[:], w1_bf[:, k, f * P : (f + 1) * P], x_bf[:, k, :],
@@ -65,55 +79,74 @@ def tile_perception_b_kernel(tc, xs, xt, w1, b1, w2, offs, out):
                 )
             return bank
 
-        def project_sources(c):
-            nc.vector.tensor_copy(xs_bf[c][:], xs_raw[c][:])
-            for f in range(BLOCKS):
-                bank = project(xs_bf[c], f)
-                ys_chunk = ys[f][:, c * CHUNK : (c + 1) * CHUNK]
-                nc.vector.tensor_copy(ys_chunk, bank[:])
-                nc.scalar.activation(hs[c][:, f, :], ys_chunk, RELU, bias=bias[:, f, :])
-
         def project_targets(c):
+            for f in range(BLOCKS):
+                nc.scalar.activation(totals[c][f][:], project(xt_bf[c], f)[:], COPY, scale=0.5)
+
+        def store(bank, m, first_column, by_vector=False):
+            result = results.tile([P, CHUNK], F32, name="result")
+            if by_vector:
+                nc.vector.tensor_copy(result[:], bank[:])
+            else:
+                nc.scalar.activation(result[:], bank[:], COPY)
+            nc.sync.dma_start(out[m * P : (m + 1) * P, first_column : first_column + CHUNK], result[:])
+
+        for k in range(BLOCKS):
+            nc.vector.tensor_copy(w1_bf[:, k, :], w1_raw[:, k, :])
+            nc.vector.tensor_copy(xt_bf[0][:, k, :], xt_raw[0][:, k, :])
+        project_targets(0)
+
+        round_by_block(xs_bf[0], xs_raw[0])
+        for c in range(CHUNKS):
+            if c + 1 < CHUNKS:
+                round_by_block(xs_bf[c + 1], xs_raw[c + 1])
+            for f in range(EARLY):
+                nc.vector.tensor_copy(ys[f][:, c * CHUNK : (c + 1) * CHUNK], project(xs_bf[c], f)[:])
+
+        for f in range(EARLY, BLOCKS):
+            for c in range(CHUNKS):
+                nc.scalar.activation(ys[f][:, c * CHUNK : (c + 1) * CHUNK], project(xs_bf[c], f)[:], COPY)
+
+        for c in range(1, CHUNKS):
             nc.scalar.activation(xt_bf[c][:], xt_raw[c][:], COPY)
-            started = []
-            for f in range(BLOCKS):
-                bank = project(xt_bf[c], f)
-                half = halves.tile([P, CHUNK], F32, name="half")
-                nc.scalar.activation(half[:], bank[:], COPY, scale=0.5)
-                started.append(half)
-            return started
+            project_targets(c)
+        nc.scalar.activation(w2_bf[:], w2_raw[:], COPY)
 
-        def aggregate(c, started):
+        for c in range(CHUNKS):
             for f in range(BLOCKS):
-                total = started[f]
+                parts = [totals[c][f][:, piece * PIECE : (piece + 1) * PIECE] for piece in range(PIECES)]
+                so_far = list(parts)
                 for r in range(SOURCES):
-                    first = (r * NODES + c * CHUNK) // 16
-                    picked = ys[f][:].indirect(offsets[:, first : first + CHUNK // 16])
-                    longer = sums.tile([P, CHUNK], F32, name="longer")
-                    nc.vector.tensor_tensor(longer[:], picked, total[:], ADD)
-                    total = longer
-                nc.scalar.activation(ht[c][:, f, :], total[:], RELU, bias=bias[:, f, :], scale=0.5)
+                    for piece in range(PIECES):
+                        first = (r * NODES + c * CHUNK + piece * PIECE) // 16
+                        picked = ys[f][:].indirect(offsets[:, first : first + PIECE // 16])
+                        if r < SOURCES - 1:
+                            longer = partials.tile([P, PIECE], F32, name="partial")[:]
+                        else:
+                            longer = parts[piece]
+                        nc.vector.tensor_tensor(longer, picked, so_far[piece], ADD)
+                        so_far[piece] = longer
 
-        def second_layer(h, first_column):
-            for m in range(BLOCKS):
-                bank = psum.tile([P, CHUNK], F32, name="product")
+        for c in range(CHUNKS):
+            for f in range(BLOCKS):
+                nc.scalar.activation(
+                    hs[c][:, f, :], ys[f][:, c * CHUNK : (c + 1) * CHUNK], RELU, bias=bias[:, f, :]
+                )
+            open_now = [open_banks.tile([P, CHUNK], F32, name=f"open{m}") for m in range(BLOCKS)]
+            for step in range(BLOCKS):
+                bank = banks.tile([P, CHUNK], F32, name="bank")
                 for f in range(BLOCKS):
                     nc.tensor.matmul(
-                        bank[:], w2_bf[:, f, m * P : (m + 1) * P], h[:, f, :],
+                        bank[:], w2_bf[:, f, step * P : (step + 1) * P], hs[c][:, f, :],
                         start=(f == 0), stop=(f == BLOCKS - 1),
                     )
-                result = results.tile([P, CHUNK], F32, name="result")
-                nc.scalar.activation(result[:], bank[:], COPY)
-                nc.sync.dma_start(out[m * P : (m + 1) * P, first_column : first_column + CHUNK], result[:])
-
-        nc.vector.tensor_copy(w1_bf[:], w1_raw[:])
-        for c in range(CHUNKS):
-            project_sources(c)
-        started = project_targets(0)
-        nc.scalar.activation(w2_bf[:], w2_raw[:], COPY)
-        for c in range(CHUNKS):
-            following = project_targets(c + 1) if c + 1 < CHUNKS else None
-            aggregate(c, started)
-            second_layer(hs[c], c * CHUNK)
-            second_layer(ht[c], NODES + c * CHUNK)
-            started = following
+                store(bank, step, c * CHUNK)
+                ht = relus.tile([P, CHUNK], BF16, name="ht")
+                nc.scalar.activation(ht[:], totals[c][step][:], RELU, bias=bias[:, step, :], scale=0.5)
+                for m in range(BLOCKS):
+                    nc.tensor.matmul(
+                        open_now[m][:], w2_bf[:, step, m * P : (m + 1) * P], ht[:],
+                        start=(step == 0), stop=(step == BLOCKS - 1),
+                    )
+            for m in range(BLOCKS):
+                store(open_now[m], m, NODES + c * CHUNK, by_vector=(c == CHUNKS - 1 and m % 2 == 1))

@@ -50,8 +50,10 @@ def tile_perception_b_kernel(tc, xs, xt, w1, b1, w2, offs, out):
         for k in range(BLOCKS):
             nc.sync.dma_start(w1_raw[:, k, :], w1_blocks[:, k, :])
             nc.sync.dma_start(xt_raw[0][:, k, :], xt_blocks[:, k, 0:CHUNK])
-        for c in range(CHUNKS):
+        for c in range(CHUNKS - 1):
             nc.sync.dma_start(xs_raw[c][:], xs_blocks[:, :, c * CHUNK : (c + 1) * CHUNK])
+        for k in range(BLOCKS):
+            nc.sync.dma_start(xs_raw[CHUNKS - 1][:, k, :], xs_blocks[:, k, NODES - CHUNK : NODES])
         for c in range(1, CHUNKS):
             nc.sync.dma_start(xt_raw[c][:], xt_blocks[:, :, c * CHUNK : (c + 1) * CHUNK])
         nc.sync.dma_start(w2_raw[:], w2_blocks)
@@ -96,12 +98,14 @@ def tile_perception_b_kernel(tc, xs, xt, w1, b1, w2, offs, out):
             nc.vector.tensor_copy(xt_bf[0][:, k, :], xt_raw[0][:, k, :])
         project_targets(0)
 
-        round_by_block(xs_bf[0], xs_raw[0])
         for c in range(CHUNKS):
-            if c + 1 < CHUNKS:
-                round_by_block(xs_bf[c + 1], xs_raw[c + 1])
+            round_by_block(xs_bf[c], xs_raw[c])
             for f in range(EARLY):
-                nc.vector.tensor_copy(ys[f][:, c * CHUNK : (c + 1) * CHUNK], project(xs_bf[c], f)[:])
+                ys_chunk = ys[f][:, c * CHUNK : (c + 1) * CHUNK]
+                if c < CHUNKS - 1:
+                    nc.scalar.activation(ys_chunk, project(xs_bf[c], f)[:], COPY)
+                else:
+                    nc.vector.tensor_copy(ys_chunk, project(xs_bf[c], f)[:])
 
         for f in range(EARLY, BLOCKS):
             for c in range(CHUNKS):

@@ -15,8 +15,6 @@ BLOCKS = FEATURES // P
 CHUNK = 512
 CHUNKS = NODES // CHUNK
 LIST = SOURCES * NODES
-PIECES = 2
-PIECE = CHUNK // PIECES
 EARLY = 2
 
 FLOPS = 2 * 2 * FEATURES * FEATURES * 2 * NODES
@@ -26,7 +24,7 @@ def tile_perception_b_kernel(tc, xs, xt, w1, b1, w2, offs, out):
     nc = tc.nc
     with (
         tc.tile_pool(name="held", bufs=1) as held,
-        tc.tile_pool(name="partials", bufs=2 * PIECES) as partials,
+        tc.tile_pool(name="partials", bufs=4) as partials,
         tc.tile_pool(name="relus", bufs=2) as relus,
         tc.tile_pool(name="results", bufs=6) as results,
         tc.psum_pool(name="banks", bufs=4) as banks,
@@ -116,20 +114,26 @@ def tile_perception_b_kernel(tc, xs, xt, w1, b1, w2, offs, out):
             project_targets(c)
         nc.scalar.activation(w2_bf[:], w2_raw[:], COPY)
 
-        for c in range(CHUNKS):
-            for f in range(BLOCKS):
-                parts = [totals[c][f][:, piece * PIECE : (piece + 1) * PIECE] for piece in range(PIECES)]
-                so_far = list(parts)
-                for r in range(SOURCES):
-                    for piece in range(PIECES):
-                        first = (r * NODES + c * CHUNK + piece * PIECE) // 16
-                        picked = ys[f][:].indirect(offsets[:, first : first + PIECE // 16])
-                        if r < SOURCES - 1:
-                            longer = partials.tile([P, PIECE], F32, name="partial")[:]
-                        else:
-                            longer = parts[piece]
-                        nc.vector.tensor_tensor(longer, picked, so_far[piece], ADD)
-                        so_far[piece] = longer
+        sums = [(c, f) for c in range(CHUNKS) for f in range(BLOCKS)]
+        so_far = {(c, f): totals[c][f][:] for c, f in sums}
+
+        def add_source(c, f, r):
+            first = (r * NODES + c * CHUNK) // 16
+            picked = ys[f][:].indirect(offsets[:, first : first + CHUNK // 16])
+            if r < SOURCES - 1:
+                longer = partials.tile([P, CHUNK], F32, name="partial")[:]
+            else:
+                longer = totals[c][f][:]
+            nc.vector.tensor_tensor(longer, picked, so_far[c, f], ADD)
+            so_far[c, f] = longer
+
+        for this, before in zip(sums + [None], [None] + sums):
+            if this:
+                add_source(*this, 0)
+            if before:
+                add_source(*before, 2)
+            if this:
+                add_source(*this, 1)
 
         for c in range(CHUNKS):
             for f in range(BLOCKS):

@@ -16,6 +16,7 @@ CHUNK = 512
 CHUNKS = NODES // CHUNK
 LIST = SOURCES * NODES
 EARLY = 2
+LAST_PIECES = 2
 
 FLOPS = 2 * 2 * FEATURES * FEATURES * 2 * NODES
 
@@ -31,7 +32,6 @@ def tile_perception_b_kernel(tc, xs, xt, w1, b1, w2, offs, out):
         tc.psum_pool(name="open_banks", bufs=1) as open_banks,
     ):
         offsets = held.tile([P, LIST // 16], U16, name="offsets")
-        nc.sync.dma_start(offsets[:], offs)
 
         bias = held.tile([P, BLOCKS, 1], F32, name="bias")
         with nc.allow_non_contiguous_dma(reason="one bias value to a partition"):
@@ -52,6 +52,7 @@ def tile_perception_b_kernel(tc, xs, xt, w1, b1, w2, offs, out):
             nc.sync.dma_start(xs_raw[c][:], xs_blocks[:, :, c * CHUNK : (c + 1) * CHUNK])
         for k in range(BLOCKS):
             nc.sync.dma_start(xs_raw[CHUNKS - 1][:, k, :], xs_blocks[:, k, NODES - CHUNK : NODES])
+        nc.sync.dma_start(offsets[:], offs)
         for c in range(1, CHUNKS):
             nc.sync.dma_start(xt_raw[c][:], xt_blocks[:, :, c * CHUNK : (c + 1) * CHUNK])
         nc.sync.dma_start(w2_raw[:], w2_blocks)
@@ -83,6 +84,17 @@ def tile_perception_b_kernel(tc, xs, xt, w1, b1, w2, offs, out):
             for f in range(BLOCKS):
                 nc.scalar.activation(totals[c][f][:], project(xt_bf[c], f)[:], COPY, scale=0.5)
 
+        def project_targets_as_they_come(c):
+            side_by_side = [banks.tile([P, CHUNK], F32, name="bank") for f in range(BLOCKS)]
+            for k in range(BLOCKS):
+                for f in range(BLOCKS):
+                    nc.tensor.matmul(
+                        side_by_side[f][:], w1_bf[:, k, f * P : (f + 1) * P], xt_bf[c][:, k, :],
+                        start=(k == 0), stop=(k == BLOCKS - 1),
+                    )
+            for f in range(BLOCKS):
+                nc.scalar.activation(totals[c][f][:], side_by_side[f][:], COPY, scale=0.5)
+
         def store(bank, m, first_column, by_vector=False):
             result = results.tile([P, CHUNK], F32, name="result")
             if by_vector:
@@ -94,16 +106,16 @@ def tile_perception_b_kernel(tc, xs, xt, w1, b1, w2, offs, out):
         for k in range(BLOCKS):
             nc.vector.tensor_copy(w1_bf[:, k, :], w1_raw[:, k, :])
             nc.vector.tensor_copy(xt_bf[0][:, k, :], xt_raw[0][:, k, :])
-        project_targets(0)
+        project_targets_as_they_come(0)
 
         for c in range(CHUNKS):
             round_by_block(xs_bf[c], xs_raw[c])
             for f in range(EARLY):
                 ys_chunk = ys[f][:, c * CHUNK : (c + 1) * CHUNK]
-                if c < CHUNKS - 1:
-                    nc.scalar.activation(ys_chunk, project(xs_bf[c], f)[:], COPY)
-                else:
+                if c == CHUNKS - 1 and f == 0:
                     nc.vector.tensor_copy(ys_chunk, project(xs_bf[c], f)[:])
+                else:
+                    nc.scalar.activation(ys_chunk, project(xs_bf[c], f)[:], COPY)
 
         for f in range(EARLY, BLOCKS):
             for c in range(CHUNKS):
@@ -117,21 +129,25 @@ def tile_perception_b_kernel(tc, xs, xt, w1, b1, w2, offs, out):
         sums = [(c, f) for c in range(CHUNKS) for f in range(BLOCKS)]
         so_far = {(c, f): totals[c][f][:] for c, f in sums}
 
-        def add_source(c, f, r):
-            first = (r * NODES + c * CHUNK) // 16
-            picked = ys[f][:].indirect(offsets[:, first : first + CHUNK // 16])
+        def pieces_of_chunk(pieces):
+            return [slice(piece * CHUNK // pieces, (piece + 1) * CHUNK // pieces) for piece in range(pieces)]
+
+        def add_source(c, f, r, pieces=1):
             if r < SOURCES - 1:
                 longer = partials.tile([P, CHUNK], F32, name="partial")[:]
             else:
                 longer = totals[c][f][:]
-            nc.vector.tensor_tensor(longer, picked, so_far[c, f], ADD)
+            for columns in pieces_of_chunk(pieces):
+                first = r * NODES + c * CHUNK + columns.start
+                picked = ys[f][:].indirect(offsets[:, first // 16 : (first + CHUNK // pieces) // 16])
+                nc.vector.tensor_tensor(longer[:, columns], picked, so_far[c, f][:, columns], ADD)
             so_far[c, f] = longer
 
         for this, before in zip(sums + [None], [None] + sums):
             if this:
                 add_source(*this, 0)
             if before:
-                add_source(*before, 2)
+                add_source(*before, 2, pieces=(1 if this else LAST_PIECES))
             if this:
                 add_source(*this, 1)
 
@@ -150,11 +166,15 @@ def tile_perception_b_kernel(tc, xs, xt, w1, b1, w2, offs, out):
                     )
                 store(bank, step, c * CHUNK)
                 ht = relus.tile([P, CHUNK], BF16, name="ht")
-                nc.scalar.activation(ht[:], totals[c][step][:], RELU, bias=bias[:, step, :], scale=0.5)
-                for m in range(BLOCKS):
-                    nc.tensor.matmul(
-                        open_now[m][:], w2_bf[:, step, m * P : (m + 1) * P], ht[:],
-                        start=(step == 0), stop=(step == BLOCKS - 1),
+                pieces = pieces_of_chunk(LAST_PIECES if (c, step) == sums[-1] else 1)
+                for columns in pieces:
+                    nc.scalar.activation(
+                        ht[:, columns], totals[c][step][:, columns], RELU, bias=bias[:, step, :], scale=0.5
                     )
+                    for m in range(BLOCKS):
+                        nc.tensor.matmul(
+                            open_now[m][:, columns], w2_bf[:, step, m * P : (m + 1) * P], ht[:, columns],
+                            start=(step == 0), stop=(step == BLOCKS - 1 and columns is pieces[-1]),
+                        )
             for m in range(BLOCKS):
                 store(open_now[m], m, NODES + c * CHUNK, by_vector=(c == CHUNKS - 1 and m % 2 == 1))

@@ -48,10 +48,12 @@ def tile_perception_b_kernel(tc, xs, xt, w1, b1, w2, offs, out):
         for k in range(BLOCKS):
             nc.sync.dma_start(w1_raw[:, k, :], w1_blocks[:, k, :])
             nc.sync.dma_start(xt_raw[0][:, k, :], xt_blocks[:, k, 0:CHUNK])
-        for c in range(CHUNKS - 1):
-            nc.sync.dma_start(xs_raw[c][:], xs_blocks[:, :, c * CHUNK : (c + 1) * CHUNK])
-        for k in range(BLOCKS):
-            nc.sync.dma_start(xs_raw[CHUNKS - 1][:, k, :], xs_blocks[:, k, NODES - CHUNK : NODES])
+        for c in range(CHUNKS):
+            if c in (0, CHUNKS - 1):
+                for k in range(BLOCKS):
+                    nc.sync.dma_start(xs_raw[c][:, k, :], xs_blocks[:, k, c * CHUNK : (c + 1) * CHUNK])
+            else:
+                nc.sync.dma_start(xs_raw[c][:], xs_blocks[:, :, c * CHUNK : (c + 1) * CHUNK])
         nc.sync.dma_start(offsets[:], offs)
         for c in range(1, CHUNKS):
             nc.sync.dma_start(xt_raw[c][:], xt_blocks[:, :, c * CHUNK : (c + 1) * CHUNK])
@@ -84,16 +86,13 @@ def tile_perception_b_kernel(tc, xs, xt, w1, b1, w2, offs, out):
             for f in range(BLOCKS):
                 nc.scalar.activation(totals[c][f][:], project(xt_bf[c], f)[:], COPY, scale=0.5)
 
-        def project_targets_as_they_come(c):
-            side_by_side = [banks.tile([P, CHUNK], F32, name="bank") for f in range(BLOCKS)]
+        def project_as_it_comes(x_bf, side_by_side):
             for k in range(BLOCKS):
                 for f in range(BLOCKS):
                     nc.tensor.matmul(
-                        side_by_side[f][:], w1_bf[:, k, f * P : (f + 1) * P], xt_bf[c][:, k, :],
+                        side_by_side[f][:], w1_bf[:, k, f * P : (f + 1) * P], x_bf[:, k, :],
                         start=(k == 0), stop=(k == BLOCKS - 1),
                     )
-            for f in range(BLOCKS):
-                nc.scalar.activation(totals[c][f][:], side_by_side[f][:], COPY, scale=0.5)
 
         def store(bank, m, first_column, by_vector=False):
             result = results.tile([P, CHUNK], F32, name="result")
@@ -106,9 +105,18 @@ def tile_perception_b_kernel(tc, xs, xt, w1, b1, w2, offs, out):
         for k in range(BLOCKS):
             nc.vector.tensor_copy(w1_bf[:, k, :], w1_raw[:, k, :])
             nc.vector.tensor_copy(xt_bf[0][:, k, :], xt_raw[0][:, k, :])
-        project_targets_as_they_come(0)
+        side_by_side = [banks.tile([P, CHUNK], F32, name="bank") for f in range(BLOCKS)]
+        project_as_it_comes(xt_bf[0], side_by_side)
+        for f in range(BLOCKS):
+            nc.scalar.activation(totals[0][f][:], side_by_side[f][:], COPY, scale=0.5)
 
-        for c in range(CHUNKS):
+        round_by_block(xs_bf[0], xs_raw[0])
+        side_by_side = [open_banks.tile([P, CHUNK], F32, name=f"open{f}") for f in range(BLOCKS)]
+        project_as_it_comes(xs_bf[0], side_by_side)
+        for f in range(BLOCKS):
+            nc.scalar.activation(ys[f][:, 0:CHUNK], side_by_side[f][:], COPY)
+
+        for c in range(1, CHUNKS):
             round_by_block(xs_bf[c], xs_raw[c])
             for f in range(EARLY):
                 ys_chunk = ys[f][:, c * CHUNK : (c + 1) * CHUNK]
@@ -118,7 +126,7 @@ def tile_perception_b_kernel(tc, xs, xt, w1, b1, w2, offs, out):
                     nc.scalar.activation(ys_chunk, project(xs_bf[c], f)[:], COPY)
 
         for f in range(EARLY, BLOCKS):
-            for c in range(CHUNKS):
+            for c in range(1, CHUNKS):
                 nc.scalar.activation(ys[f][:, c * CHUNK : (c + 1) * CHUNK], project(xs_bf[c], f)[:], COPY)
 
         for c in range(1, CHUNKS):
@@ -157,24 +165,27 @@ def tile_perception_b_kernel(tc, xs, xt, w1, b1, w2, offs, out):
                     hs[c][:, f, :], ys[f][:, c * CHUNK : (c + 1) * CHUNK], RELU, bias=bias[:, f, :]
                 )
             open_now = [open_banks.tile([P, CHUNK], F32, name=f"open{m}") for m in range(BLOCKS)]
-            for step in range(BLOCKS):
-                bank = banks.tile([P, CHUNK], F32, name="bank")
-                for f in range(BLOCKS):
-                    nc.tensor.matmul(
-                        bank[:], w2_bf[:, f, step * P : (step + 1) * P], hs[c][:, f, :],
-                        start=(f == 0), stop=(f == BLOCKS - 1),
-                    )
-                store(bank, step, c * CHUNK)
-                ht = relus.tile([P, CHUNK], BF16, name="ht")
-                pieces = pieces_of_chunk(LAST_PIECES if (c, step) == sums[-1] else 1)
-                for columns in pieces:
-                    nc.scalar.activation(
-                        ht[:, columns], totals[c][step][:, columns], RELU, bias=bias[:, step, :], scale=0.5
-                    )
-                    for m in range(BLOCKS):
+            for step in range(BLOCKS + 1):
+                if step < BLOCKS:
+                    bank = banks.tile([P, CHUNK], F32, name="bank")
+                    for f in range(BLOCKS):
                         nc.tensor.matmul(
-                            open_now[m][:, columns], w2_bf[:, step, m * P : (m + 1) * P], ht[:, columns],
-                            start=(step == 0), stop=(step == BLOCKS - 1 and columns is pieces[-1]),
+                            bank[:], w2_bf[:, f, step * P : (step + 1) * P], hs[c][:, f, :],
+                            start=(f == 0), stop=(f == BLOCKS - 1),
                         )
+                    store(bank, step, c * CHUNK)
+                if step > 0:
+                    f = step - 1
+                    ht = relus.tile([P, CHUNK], BF16, name="ht")
+                    pieces = pieces_of_chunk(LAST_PIECES if (c, f) == sums[-1] else 1)
+                    for columns in pieces:
+                        nc.scalar.activation(
+                            ht[:, columns], totals[c][f][:, columns], RELU, bias=bias[:, f, :], scale=0.5
+                        )
+                        for m in range(BLOCKS):
+                            nc.tensor.matmul(
+                                open_now[m][:, columns], w2_bf[:, f, m * P : (m + 1) * P], ht[:, columns],
+                                start=(f == 0), stop=(f == BLOCKS - 1 and columns is pieces[-1]),
+                            )
             for m in range(BLOCKS):
                 store(open_now[m], m, NODES + c * CHUNK, by_vector=(c == CHUNKS - 1 and m % 2 == 1))

@@ -116,18 +116,24 @@ def tile_perception_b_kernel(tc, xs, xt, w1, b1, w2, offs, out):
         for f in range(BLOCKS):
             nc.scalar.activation(ys[f][:, 0:CHUNK], side_by_side[f][:], COPY)
 
+        def project_sources(f, c, by_vector=False):
+            ys_chunk = ys[f][:, c * CHUNK : (c + 1) * CHUNK]
+            if by_vector:
+                nc.vector.tensor_copy(ys_chunk, project(xs_bf[c], f)[:])
+            else:
+                nc.scalar.activation(ys_chunk, project(xs_bf[c], f)[:], COPY)
+
         for c in range(1, CHUNKS):
             round_by_block(xs_bf[c], xs_raw[c])
-            for f in range(EARLY):
-                ys_chunk = ys[f][:, c * CHUNK : (c + 1) * CHUNK]
-                if c == CHUNKS - 1 and f == 0:
-                    nc.vector.tensor_copy(ys_chunk, project(xs_bf[c], f)[:])
-                else:
-                    nc.scalar.activation(ys_chunk, project(xs_bf[c], f)[:], COPY)
-
+        for f in range(EARLY):
+            project_sources(f, 1)
+        project_sources(0, CHUNKS - 2)
+        project_sources(0, CHUNKS - 1, by_vector=True)
+        project_sources(1, CHUNKS - 2)
+        project_sources(1, CHUNKS - 1)
         for f in range(EARLY, BLOCKS):
             for c in range(1, CHUNKS):
-                nc.scalar.activation(ys[f][:, c * CHUNK : (c + 1) * CHUNK], project(xs_bf[c], f)[:], COPY)
+                project_sources(f, c)
 
         for c in range(1, CHUNKS):
             nc.scalar.activation(xt_bf[c][:], xt_raw[c][:], COPY)

@@ -4,6 +4,7 @@ F32 = mybir.dt.float32
 BF16 = mybir.dt.bfloat16
 U16 = mybir.dt.uint16
 ADD = mybir.AluOpType.add
+MAX = mybir.AluOpType.max
 RELU = mybir.ActivationFunctionType.Relu
 COPY = mybir.ActivationFunctionType.Copy
 
@@ -127,7 +128,12 @@ def tile_perception_b_kernel(tc, xs, xt, w1, b1, w2, offs, out):
             round_by_block(xs_bf[c], xs_raw[c])
         for f in range(EARLY):
             project_sources(f, 1)
+        made_early = [(0, f) for f in range(BLOCKS)] + [(1, f) for f in range(EARLY)]
         project_sources(0, CHUNKS - 2)
+        for c, f in made_early:
+            nc.vector.tensor_scalar(
+                hs[c][:, f, :], ys[f][:, c * CHUNK : (c + 1) * CHUNK], bias[:, f, :], 0.0, ADD, MAX
+            )
         project_sources(0, CHUNKS - 1, by_vector=True)
         project_sources(1, CHUNKS - 2)
         project_sources(1, CHUNKS - 1)
@@ -167,9 +173,10 @@ def tile_perception_b_kernel(tc, xs, xt, w1, b1, w2, offs, out):
 
         for c in range(CHUNKS):
             for f in range(BLOCKS):
-                nc.scalar.activation(
-                    hs[c][:, f, :], ys[f][:, c * CHUNK : (c + 1) * CHUNK], RELU, bias=bias[:, f, :]
-                )
+                if (c, f) not in made_early:
+                    nc.scalar.activation(
+                        hs[c][:, f, :], ys[f][:, c * CHUNK : (c + 1) * CHUNK], RELU, bias=bias[:, f, :]
+                    )
             open_now = [open_banks.tile([P, CHUNK], F32, name=f"open{m}") for m in range(BLOCKS)]
             for step in range(BLOCKS + 1):
                 if step < BLOCKS:

@@ -49,12 +49,11 @@ def tile_perception_b_kernel(tc, xs, xt, w1, b1, w2, offs, out):
         for k in range(BLOCKS):
             nc.sync.dma_start(w1_raw[:, k, :], w1_blocks[:, k, :])
             nc.sync.dma_start(xt_raw[0][:, k, :], xt_blocks[:, k, 0:CHUNK])
-        for c in range(CHUNKS):
-            if c in (0, CHUNKS - 1):
-                for k in range(BLOCKS):
-                    nc.sync.dma_start(xs_raw[c][:, k, :], xs_blocks[:, k, c * CHUNK : (c + 1) * CHUNK])
-            else:
-                nc.sync.dma_start(xs_raw[c][:], xs_blocks[:, :, c * CHUNK : (c + 1) * CHUNK])
+            nc.sync.dma_start(xs_raw[0][:, k, :], xs_blocks[:, k, 0:CHUNK])
+        for c in range(1, CHUNKS - 1):
+            nc.sync.dma_start(xs_raw[c][:], xs_blocks[:, :, c * CHUNK : (c + 1) * CHUNK])
+        for k in range(BLOCKS):
+            nc.sync.dma_start(xs_raw[CHUNKS - 1][:, k, :], xs_blocks[:, k, NODES - CHUNK : NODES])
         nc.sync.dma_start(offsets[:], offs)
         for c in range(1, CHUNKS):
             nc.sync.dma_start(xt_raw[c][:], xt_blocks[:, :, c * CHUNK : (c + 1) * CHUNK])
@@ -87,14 +86,6 @@ def tile_perception_b_kernel(tc, xs, xt, w1, b1, w2, offs, out):
             for f in range(BLOCKS):
                 nc.scalar.activation(totals[c][f][:], project(xt_bf[c], f)[:], COPY, scale=0.5)
 
-        def project_as_it_comes(x_bf, side_by_side):
-            for k in range(BLOCKS):
-                for f in range(BLOCKS):
-                    nc.tensor.matmul(
-                        side_by_side[f][:], w1_bf[:, k, f * P : (f + 1) * P], x_bf[:, k, :],
-                        start=(k == 0), stop=(k == BLOCKS - 1),
-                    )
-
         def store(bank, m, first_column, by_vector=False):
             result = results.tile([P, CHUNK], F32, name="result")
             if by_vector:
@@ -103,19 +94,21 @@ def tile_perception_b_kernel(tc, xs, xt, w1, b1, w2, offs, out):
                 nc.scalar.activation(result[:], bank[:], COPY)
             nc.sync.dma_start(out[m * P : (m + 1) * P, first_column : first_column + CHUNK], result[:])
 
+        yt_banks = [banks.tile([P, CHUNK], F32, name="bank") for f in range(BLOCKS)]
+        ys_banks = [open_banks.tile([P, CHUNK], F32, name=f"open{f}") for f in range(BLOCKS)]
         for k in range(BLOCKS):
             nc.vector.tensor_copy(w1_bf[:, k, :], w1_raw[:, k, :])
-            nc.vector.tensor_copy(xt_bf[0][:, k, :], xt_raw[0][:, k, :])
-        side_by_side = [banks.tile([P, CHUNK], F32, name="bank") for f in range(BLOCKS)]
-        project_as_it_comes(xt_bf[0], side_by_side)
+            for x_bf, x_raw, side_by_side in ((xt_bf[0], xt_raw[0], yt_banks), (xs_bf[0], xs_raw[0], ys_banks)):
+                nc.vector.tensor_copy(x_bf[:, k, :], x_raw[:, k, :])
+                for f in range(BLOCKS):
+                    nc.tensor.matmul(
+                        side_by_side[f][:], w1_bf[:, k, f * P : (f + 1) * P], x_bf[:, k, :],
+                        start=(k == 0), stop=(k == BLOCKS - 1),
+                    )
         for f in range(BLOCKS):
-            nc.scalar.activation(totals[0][f][:], side_by_side[f][:], COPY, scale=0.5)
-
-        round_by_block(xs_bf[0], xs_raw[0])
-        side_by_side = [open_banks.tile([P, CHUNK], F32, name=f"open{f}") for f in range(BLOCKS)]
-        project_as_it_comes(xs_bf[0], side_by_side)
+            nc.scalar.activation(totals[0][f][:], yt_banks[f][:], COPY, scale=0.5)
         for f in range(BLOCKS):
-            nc.scalar.activation(ys[f][:, 0:CHUNK], side_by_side[f][:], COPY)
+            nc.scalar.activation(ys[f][:, 0:CHUNK], ys_banks[f][:], COPY)
 
         def project_sources(f, c, by_vector=False):
             ys_chunk = ys[f][:, c * CHUNK : (c + 1) * CHUNK]

import concourse.mybir as mybir

F32 = mybir.dt.float32
BF16 = mybir.dt.bfloat16
U16 = mybir.dt.uint16
ADD = mybir.AluOpType.add
MAX = mybir.AluOpType.max
RELU = mybir.ActivationFunctionType.Relu
COPY = mybir.ActivationFunctionType.Copy

P = 128
FEATURES = 512
NODES = 2048
SOURCES = 3
BLOCKS = FEATURES // P
CHUNK = 512
CHUNKS = NODES // CHUNK
LIST = SOURCES * NODES
EARLY = 2
LAST_PIECES = 2

FLOPS = 2 * 2 * FEATURES * FEATURES * 2 * NODES


def tile_perception_b_kernel(tc, xs, xt, w1, b1, w2, offs, out):
    nc = tc.nc
    with (
        tc.tile_pool(name="held", bufs=1) as held,
        tc.tile_pool(name="partials", bufs=4) as partials,
        tc.tile_pool(name="relus", bufs=2) as relus,
        tc.tile_pool(name="results", bufs=6) as results,
        tc.psum_pool(name="banks", bufs=4) as banks,
        tc.psum_pool(name="open_banks", bufs=1) as open_banks,
    ):
        offsets = held.tile([P, LIST // 16], U16, name="offsets")

        bias = held.tile([P, BLOCKS, 1], F32, name="bias")
        with nc.allow_non_contiguous_dma(reason="one bias value to a partition"):
            nc.scalar.dma_start(bias[:], b1.rearrange("(f p) o -> p f o", p=P))

        w1_blocks = w1.rearrange("(k p) f -> p k f", p=P)
        w2_blocks = w2.rearrange("(f p) m -> p f m", p=P)
        xs_blocks = xs.rearrange("(k p) s -> p k s", p=P)
        xt_blocks = xt.rearrange("(k p) t -> p k t", p=P)
        w1_raw = held.tile([P, BLOCKS, FEATURES], F32, name="w1_raw")
        w2_raw = held.tile([P, BLOCKS, FEATURES], F32, name="w2_raw")
        xs_raw = [held.tile([P, BLOCKS, CHUNK], F32, name=f"xs_raw{c}") for c in range(CHUNKS)]
        xt_raw = [held.tile([P, BLOCKS, CHUNK], F32, name=f"xt_raw{c}") for c in range(CHUNKS)]
        for k in range(BLOCKS):
            nc.sync.dma_start(w1_raw[:, k, :], w1_blocks[:, k, :])
            nc.sync.dma_start(xt_raw[0][:, k, :], xt_blocks[:, k, 0:CHUNK])
            nc.sync.dma_start(xs_raw[0][:, k, :], xs_blocks[:, k, 0:CHUNK])
        for c in range(1, CHUNKS - 1):
            nc.sync.dma_start(xs_raw[c][:], xs_blocks[:, :, c * CHUNK : (c + 1) * CHUNK])
        for k in range(BLOCKS):
            nc.sync.dma_start(xs_raw[CHUNKS - 1][:, k, :], xs_blocks[:, k, NODES - CHUNK : NODES])
        nc.sync.dma_start(offsets[:], offs)
        for c in range(1, CHUNKS):
            nc.sync.dma_start(xt_raw[c][:], xt_blocks[:, :, c * CHUNK : (c + 1) * CHUNK])
        nc.sync.dma_start(w2_raw[:], w2_blocks)

        w1_bf = held.tile([P, BLOCKS, FEATURES], BF16, name="w1_bf")
        w2_bf = held.tile([P, BLOCKS, FEATURES], BF16, name="w2_bf")
        xs_bf = [held.tile([P, BLOCKS, CHUNK], BF16, name=f"xs_bf{c}") for c in range(CHUNKS)]
        xt_bf = [held.tile([P, BLOCKS, CHUNK], BF16, name=f"xt_bf{c}") for c in range(CHUNKS)]
        hs = [held.tile([P, BLOCKS, CHUNK], BF16, name=f"hs{c}") for c in range(CHUNKS)]
        ys = [held.tile([P, NODES], F32, name=f"ys{f}") for f in range(BLOCKS)]
        totals = [
            [held.tile([P, CHUNK], F32, name=f"total{c}_{f}") for f in range(BLOCKS)] for c in range(CHUNKS)
        ]

        def round_by_block(rounded, raw):
            for k in range(BLOCKS):
                nc.vector.tensor_copy(rounded[:, k, :], raw[:, k, :])

        def project(x_bf, f):
            bank = banks.tile([P, CHUNK], F32, name="bank")
            for k in range(BLOCKS):
                nc.tensor.matmul(
                    bank[:], w1_bf[:, k, f * P : (f + 1) * P], x_bf[:, k, :],
                    start=(k == 0), stop=(k == BLOCKS - 1),
                )
            return bank

        def project_targets(c):
            for f in range(BLOCKS):
                nc.scalar.activation(totals[c][f][:], project(xt_bf[c], f)[:], COPY, scale=0.5)

        def store(bank, m, first_column, by_vector=False):
            result = results.tile([P, CHUNK], F32, name="result")
            if by_vector:
                nc.vector.tensor_copy(result[:], bank[:])
            else:
                nc.scalar.activation(result[:], bank[:], COPY)
            nc.sync.dma_start(out[m * P : (m + 1) * P, first_column : first_column + CHUNK], result[:])

        yt_banks = [banks.tile([P, CHUNK], F32, name="bank") for f in range(BLOCKS)]
        ys_banks = [open_banks.tile([P, CHUNK], F32, name=f"open{f}") for f in range(BLOCKS)]
        for k in range(BLOCKS):
            nc.vector.tensor_copy(w1_bf[:, k, :], w1_raw[:, k, :])
            for x_bf, x_raw, side_by_side in ((xt_bf[0], xt_raw[0], yt_banks), (xs_bf[0], xs_raw[0], ys_banks)):
                nc.vector.tensor_copy(x_bf[:, k, :], x_raw[:, k, :])
                for f in range(BLOCKS):
                    nc.tensor.matmul(
                        side_by_side[f][:], w1_bf[:, k, f * P : (f + 1) * P], x_bf[:, k, :],
                        start=(k == 0), stop=(k == BLOCKS - 1),
                    )
        for f in range(BLOCKS):
            nc.scalar.activation(totals[0][f][:], yt_banks[f][:], COPY, scale=0.5)
        for f in range(BLOCKS):
            nc.scalar.activation(ys[f][:, 0:CHUNK], ys_banks[f][:], COPY)

        def project_sources(f, c, by_vector=False):
            ys_chunk = ys[f][:, c * CHUNK : (c + 1) * CHUNK]
            if by_vector:
                nc.vector.tensor_copy(ys_chunk, project(xs_bf[c], f)[:])
            else:
                nc.scalar.activation(ys_chunk, project(xs_bf[c], f)[:], COPY)

        for c in range(1, CHUNKS):
            round_by_block(xs_bf[c], xs_raw[c])
        for f in range(EARLY):
            project_sources(f, 1)
        made_early = [(0, f) for f in range(BLOCKS)] + [(1, f) for f in range(EARLY)]
        project_sources(0, CHUNKS - 2)
        for c, f in made_early:
            nc.vector.tensor_scalar(
                hs[c][:, f, :], ys[f][:, c * CHUNK : (c + 1) * CHUNK], bias[:, f, :], 0.0, ADD, MAX
            )
        project_sources(0, CHUNKS - 1, by_vector=True)
        project_sources(1, CHUNKS - 2)
        project_sources(1, CHUNKS - 1)
        for f in range(EARLY, BLOCKS):
            for c in range(1, CHUNKS):
                project_sources(f, c)

        for c in range(1, CHUNKS):
            nc.scalar.activation(xt_bf[c][:], xt_raw[c][:], COPY)
            project_targets(c)
        nc.scalar.activation(w2_bf[:], w2_raw[:], COPY)

        sums = [(c, f) for c in range(CHUNKS) for f in range(BLOCKS)]
        so_far = {(c, f): totals[c][f][:] for c, f in sums}

        def pieces_of_chunk(pieces):
            return [slice(piece * CHUNK // pieces, (piece + 1) * CHUNK // pieces) for piece in range(pieces)]

        def add_source(c, f, r, pieces=1):
            if r < SOURCES - 1:
                longer = partials.tile([P, CHUNK], F32, name="partial")[:]
            else:
                longer = totals[c][f][:]
            for columns in pieces_of_chunk(pieces):
                first = r * NODES + c * CHUNK + columns.start
                picked = ys[f][:].indirect(offsets[:, first // 16 : (first + CHUNK // pieces) // 16])
                nc.vector.tensor_tensor(longer[:, columns], picked, so_far[c, f][:, columns], ADD)
            so_far[c, f] = longer

        for this, before in zip(sums + [None], [None] + sums):
            if this:
                add_source(*this, 0)
            if before:
                add_source(*before, 2, pieces=(1 if this else LAST_PIECES))
            if this:
                add_source(*this, 1)

        for c in range(CHUNKS):
            for f in range(BLOCKS):
                if (c, f) not in made_early:
                    nc.scalar.activation(
                        hs[c][:, f, :], ys[f][:, c * CHUNK : (c + 1) * CHUNK], RELU, bias=bias[:, f, :]
                    )
            open_now = [open_banks.tile([P, CHUNK], F32, name=f"open{m}") for m in range(BLOCKS)]
            for step in range(BLOCKS + 1):
                if step < BLOCKS:
                    bank = banks.tile([P, CHUNK], F32, name="bank")
                    for f in range(BLOCKS):
                        nc.tensor.matmul(
                            bank[:], w2_bf[:, f, step * P : (step + 1) * P], hs[c][:, f, :],
                            start=(f == 0), stop=(f == BLOCKS - 1),
                        )
                    store(bank, step, c * CHUNK)
                if step > 0:
                    f = step - 1
                    ht = relus.tile([P, CHUNK], BF16, name="ht")
                    pieces = pieces_of_chunk(LAST_PIECES if (c, f) == sums[-1] else 1)
                    for columns in pieces:
                        nc.scalar.activation(
                            ht[:, columns], totals[c][f][:, columns], RELU, bias=bias[:, f, :], scale=0.5
                        )
                        for m in range(BLOCKS):
                            nc.tensor.matmul(
                                open_now[m][:, columns], w2_bf[:, f, m * P : (m + 1) * P], ht[:, columns],
                                start=(f == 0), stop=(f == BLOCKS - 1 and columns is pieces[-1]),
                            )
            for m in range(BLOCKS):
                store(open_now[m], m, NODES + c * CHUNK, by_vector=(c == CHUNKS - 1 and m % 2 == 1))
